import numpy as np
import ml_dtypes


def mxq(x, axis, fmt="e4m3"):
    dtype, down = {"e4m3": (ml_dtypes.float8_e4m3fn, 7), "e5m2": (ml_dtypes.float8_e5m2, 14)}[fmt]
    v = np.moveaxis(np.asarray(x, np.float32).astype(ml_dtypes.bfloat16).astype(np.float64), axis, -1)
    blocks = v.reshape(v.shape[:-1] + (-1, 32))
    amax = np.abs(blocks).max(-1, keepdims=True)
    byte = np.maximum(np.where(amax > 0, np.frexp(amax)[1] - 1 + 127, 0) - down, 1)
    scale = np.exp2(byte - 127.0)
    codes = (blocks / scale).astype(np.float32).astype(dtype).astype(np.float64)
    return np.moveaxis((codes * scale).reshape(v.shape), -1, axis)


WIDE = False


def mx_kscale(k):
    if not WIDE:
        return np.ones(k)
    levels = np.array([10, -10, 5, -5, 0])
    if k % 512:
        return np.exp2(np.random.permutation(np.resize(levels, k // 32))).repeat(32)
    a = np.empty((k // 512, 16))
    for p in range(k // 512):
        a[p, :8] = np.random.permutation(np.resize(levels, 8))
        for g in range(8):
            far = levels[np.abs(levels - a[p, g]) >= 10]
            a[p, g + 8] = far[np.random.randint(len(far))]
    return np.exp2(a.ravel()).repeat(32)


BF16 = ml_dtypes.bfloat16


def bf(x):
    return np.asarray(x, np.float32).astype(BF16)


def f64(x):
    return np.asarray(x).astype(np.float64)


B, S, DIM, H, HD = 4, 128, 2048, 16, 128
E = H * HD


def rope_tables():
    inv_freq = 1.0 / (10000.0 ** (np.arange(0, HD, 2) / HD))
    freqs = np.outer(np.arange(S), inv_freq)
    emb = np.concatenate([freqs, freqs], axis=-1)
    return np.cos(emb)[None, None], np.sin(emb)[None, None]


def rotate_half(x):
    x1, x2 = np.split(x, 2, axis=-1)
    return np.concatenate([-x2, x1], axis=-1)


def draw0():
    s = mx_kscale(DIM)
    cos, sin = rope_tables()
    return {"query": bf(np.random.standard_normal((B, S, DIM)) * s),
            "wq": bf(np.random.standard_normal((E, DIM)) / np.sqrt(DIM) / s),
            "bq": bf(np.random.standard_normal(E) * 0.1),
            "cos": bf(cos), "sin": bf(sin)}


def core(query, wq, bq, cos, sin):
    q = (mxq(f64(query), 2, "e4m3") @ mxq(f64(wq), 1, "e4m3").T) + f64(bq)
    q = q.reshape(B, S, H, HD).transpose(0, 2, 1, 3)
    return q * f64(cos) + rotate_half(q) * f64(sin)


def e4m3fn_bytes(y):
    return np.clip(np.asarray(y, np.float64), -448.0, 448.0).astype(np.float32).astype(ml_dtypes.float8_e4m3fn).view(np.uint8)


def e4m3fn_values(b):
    return np.asarray(b, np.uint8).view(ml_dtypes.float8_e4m3fn).astype(np.float64)


def setup_inputs():
    d = draw0()
    x0 = np.asarray(d['wq']).astype(np.float64)
    s = (np.max(np.abs(x0), axis=(0,), keepdims=True) / 448.0).astype(np.float32)
    out = {}
    for k, v in d.items():
        if k == 'wq':
            out['wq_bytes'] = e4m3fn_bytes(x0 / s.astype(np.float64))
            out['wq_scale'] = s
        else:
            out[k] = v
    return out


def reference(query, wq_bytes, wq_scale, bq, cos, sin):
    return core(query, e4m3fn_values(wq_bytes) * wq_scale.astype(np.float64), bq, cos, sin)

@@ -1,0 +1,299 @@
+from contextlib import ExitStack
+
+import concourse.mybir as mybir
+from concourse.masks import make_identity
+
+FLOPS = 2 * 512 * 2048 * 2048
+
+F32 = mybir.dt.float32
+BF16 = mybir.dt.bfloat16
+U32 = mybir.dt.uint32
+U8 = mybir.dt.uint8
+FP8 = mybir.dt.float8_e4m3fn
+FP8X4 = mybir.dt.float8_e4m3fn_x4
+ALU = mybir.AluOpType
+ACT = mybir.ActivationFunctionType
+
+P = 128
+B = 4
+H = 16
+K = 2048
+G = 4
+TOK = 512
+HR = 14
+NX = 2
+
+
+def tile_attention_pa_kernel(tc, query, wq_bytes, wq_scale, bq, cos, sin, out):
+    nc = tc.nc
+    with ExitStack() as ctx:
+        const = ctx.enter_context(tc.tile_pool(name="const", bufs=1))
+        work = ctx.enter_context(tc.tile_pool(name="work", bufs=3))
+        psum = ctx.enter_context(tc.psum_pool(name="psum", bufs=2))
+
+        ctx.enter_context(tc.manual_schedule())
+
+        wq_bytes_sb = const.tile([P, H, K], U8, name="wq_bytes_sb")
+        scl = const.tile([P, K], F32, name="scl")
+        xq = const.tile([P, B, K], BF16, name="xq")
+        craw = const.tile([P, 3, P], BF16, name="craw")
+        scale_row = wq_scale.rearrange("o k -> (o k)")
+
+        def load_scl(c0, c1):
+            nc.scalar.dma_start(out=scl[:, c0:c1], in_=scale_row[c0:c1].partition_broadcast(P))
+
+        def load_w(h, c0=0, c1=K):
+            nc.sync.dma_start(out=wq_bytes_sb[:, h, c0:c1], in_=wq_bytes[h * P : (h + 1) * P, c0:c1])
+
+        def load_q(b, gp):
+            cs = slice(gp * 1024, (gp + 1) * 1024)
+            nc.sync.dma_start(out=xq[:, b, cs], in_=query[b, :, cs])
+
+        load_scl(0, K)
+        load_w(0)
+        load_w(1)
+        for b in range(B):
+            load_q(b, 0)
+        load_w(2)
+        for b in range(B):
+            load_q(b, 1)
+        for h in (3, 4, HR, HR + 1):
+            load_w(h)
+        for h in range(5, HR):
+            load_w(h)
+        nc.gpsimd.memset(craw[:, 2, :], 0.0)
+        nc.scalar.dma_start(out=craw[:, 0, :], in_=cos[0, 0])
+        nc.scalar.dma_start(out=craw[:, 1, :], in_=sin[0, 0])
+        nc.scalar.dma_start(out=craw[0:H, 2, :], in_=bq.rearrange("(h d) -> h d", d=P))
+        scl_t = const.tile([P, G, 4], F32, name="scl_t")
+        nc.scalar.dma_start(out=scl_t[:], in_=wq_scale.rearrange("o (g p t) -> p (o g) t", p=P, t=4))
+
+        ident = const.tile([P, P], F32, name="ident")
+        make_identity(nc, ident[:])
+        perm = const.tile([P, P], F32, name="perm")
+        nc.gpsimd.tensor_copy(out=perm[:, 0:64], in_=ident[:, 64:128])
+        nc.gpsimd.tensor_copy(out=perm[:, 64:128], in_=ident[:, 0:64])
+        stg = const.tile([P, 3, P], F32, name="stg")
+        tab = const.tile([P, 3, P], F32, name="tab")
+
+        def tables_raw():
+            nc.scalar.copy(out=stg[:, 0, :], in_=craw[:, 0, :])
+            nc.scalar.copy(out=stg[:, 1, 0:64], in_=craw[:, 1, 64:128])
+            nc.scalar.activation(out=stg[:, 1, 64:128], in_=craw[:, 1, 0:64], func=ACT.Copy, scale=-1.0)
+            nc.scalar.copy(out=stg[:, 2, :], in_=craw[:, 2, :])
+
+        def tables():
+            tps = psum.tile([P, 512], F32, name="tps", tag="tw", bufs=3)
+            for i in range(3):
+                nc.tensor.transpose(tps[:, i * P : (i + 1) * P], stg[:, i, :], ident[:])
+            nc.scalar.copy(out=tab[:].rearrange("p a s -> p (a s)"), in_=tps[:, 0 : 3 * P])
+
+        qg = const.tile([P, G * TOK * 4], BF16, name="qg", align_bytes=64)
+        qcodes = const.tile([P, G * TOK], U32, name="qcodes", align_bytes=64)
+        qscales = const.tile([P, G * TOK], U8, name="qscales", align_bytes=64)
+        wcodes = const.tile([P, HR, G * P], U32, name="wcodes", align_bytes=64)
+        wscales = const.tile([P, HR, G * P], U8, name="wscales", align_bytes=64)
+        qg_words = qg[:].bitcast(F32).rearrange("p (g n u) -> p g n u", g=G, n=TOK, u=2)
+
+        def transpose_pair(words, gp):
+            tw = psum.tile([P, 512], F32, name="tw", tag="tw", bufs=3)
+            for g2 in range(2):
+                g = 2 * gp + g2
+                for u in range(2):
+                    nc.tensor.transpose(
+                        tw[:, (2 * g2 + u) * P : (2 * g2 + u + 1) * P],
+                        words[:, 256 * g + u : 256 * (g + 1) : 2],
+                        ident[:],
+                    )
+            return tw[:].rearrange("p (g u r) -> p g r u", g=2, u=2)
+
+        wb_of = {}
+        wg_of = {}
+        acc_of = {}
+        uw_of = {}
+        ot_of = {}
+
+        def product(h):
+            wb_of[h] = work.tile([P, K], BF16, name="wb", tag="wb")
+            cuts = (0, 2048)
+            for c0, c1 in zip(cuts[:-1], cuts[1:]):
+                nc.vector.tensor_tensor(
+                    out=wb_of[h][:, c0:c1],
+                    in0=wq_bytes_sb[:, h, c0:c1].bitcast(FP8),
+                    in1=scl[:, c0:c1],
+                    op=ALU.mult,
+                )
+
+        def turn_w(h, gp):
+            if gp == 0:
+                wg_of[h] = work.tile([P, K], BF16, name="wg", tag="wg", align_bytes=64)
+            wg_words = wg_of[h][:].bitcast(F32).rearrange("p (g r u) -> p g r u", g=G, u=2)
+            src = transpose_pair(wb_of[h][:].bitcast(F32), gp)
+            nc.scalar.copy(out=wg_words[:, 2 * gp : 2 * gp + 2, :, :], in_=src)
+
+        def turn_q(b, gp):
+            src = transpose_pair(xq[:, b, :].bitcast(F32), gp)
+            nc.scalar.copy(out=qg_words[:, 2 * gp : 2 * gp + 2, b * P : (b + 1) * P, :], in_=src)
+
+        def quant_q(g):
+            nc.vector.quantize_mx(
+                out=qcodes[:, g * TOK : (g + 1) * TOK].bitcast(FP8X4),
+                scales=qscales[:, g * TOK : (g + 1) * TOK],
+                in_=qg[:, g * TOK * 4 : (g + 1) * TOK * 4],
+            )
+
+        def quant_w(h):
+            nc.vector.quantize_mx(
+                out=wcodes[:, h, :].bitcast(FP8X4), scales=wscales[:, h, :], in_=wg_of[h][:]
+            )
+
+        def codes_of(h, g):
+            if h < HR:
+                return wcodes[:, h, g * P : (g + 1) * P]
+            return xcodes[:, g * NX * P + (h - HR) * P : g * NX * P + (h - HR + 1) * P]
+
+        def scales_of(h, g):
+            if h < HR:
+                return wscales[:, h, g * P : (g + 1) * P]
+            return xscales[:, g * NX * P + (h - HR) * P : g * NX * P + (h - HR + 1) * P]
+
+        def multiply(h, passes=(0, 1, 2, 3)):
+            if passes[0] == 0:
+                acc_of[h] = psum.tile([P, TOK], F32, name="acc", tag="acc", bufs=3)
+            for g in passes:
+                nc.tensor.matmul_mx(
+                    out=acc_of[h][:],
+                    lhsT=codes_of(h, g).bitcast(FP8X4),
+                    lhsT_scale=scales_of(h, g),
+                    rhs=qcodes[:, g * TOK : (g + 1) * TOK].bitcast(FP8X4),
+                    rhs_scale=qscales[:, g * TOK : (g + 1) * TOK],
+                    start=(g == 0),
+                    stop=(g == G - 1),
+                )
+
+        def rope(h, b0, nb):
+            cs = slice(b0 * P, (b0 + nb) * P)
+            uu = work.tile([P, nb * P], F32, name="uu", tag="uu")
+            ww = work.tile([P, nb * P], F32, name="ww", tag="ww")
+            for dst, a in ((uu, 0), (ww, 1)):
+                nc.vector.scalar_tensor_tensor(
+                    out=dst[:].rearrange("p (b s) -> p b s", b=nb),
+                    in0=acc_of[h][:, cs].rearrange("p (b s) -> p b s", b=nb),
+                    scalar=tab[:, 2, h : h + 1],
+                    in1=tab[:, a, :].unsqueeze(1).to_broadcast([P, nb, P]),
+                    op0=ALU.add,
+                    op1=ALU.mult,
+                )
+            uw_of[(h, b0)] = (uu, ww)
+
+        def turn_back(h, b0, nb):
+            uu, ww = uw_of[(h, b0)]
+            ot = psum.tile([P, nb * P], F32, name="ot", tag="ot", bufs=2)
+            for b in range(nb):
+                cs = slice(b * P, (b + 1) * P)
+                nc.tensor.matmul(
+                    out=ot[:, cs], lhsT=uu[:, cs], rhs=ident[:], is_transpose=True, start=True, stop=False
+                )
+                nc.tensor.matmul(
+                    out=ot[:, cs], lhsT=ww[:, cs], rhs=perm[:], is_transpose=True, start=False, stop=True
+                )
+            osb = work.tile([P, nb * P], F32, name="osb", tag="osb", bufs=6)
+            nc.scalar.copy(out=osb[:], in_=ot[:])
+            nc.sync.dma_start(
+                out=out[b0 : b0 + nb, h, :, :].rearrange("b s d -> s b d"),
+                in_=osb[:].rearrange("p (b d) -> p b d", b=nb),
+            )
+
+        XC = NX * P
+        planes = const.tile([P, G, 4, XC], BF16, name="planes")
+        xg = const.tile([P, G * XC * 4], BF16, name="xg", align_bytes=64)
+        xcodes = const.tile([P, G * XC], U32, name="xcodes", align_bytes=64)
+        xscales = const.tile([P, G * XC], U8, name="xscales", align_bytes=64)
+        xg_view = xg[:].rearrange("p (g c t) -> p g c t", g=G, t=4)
+        wc_of = {}
+
+        def widen(r):
+            wc_of[r] = const.tile([P, K], BF16, name="wc%d" % r)
+            nc.scalar.copy(out=wc_of[r][:], in_=wq_bytes_sb[:, HR + r, :].bitcast(FP8))
+
+        def turn_x(g):
+            tw = psum.tile([P, 512], F32, name="tw", tag="tw", bufs=3)
+            for u in range(2):
+                for r in range(NX):
+                    nc.tensor.transpose(
+                        tw[:, (u * NX + r) * P : (u * NX + r + 1) * P],
+                        wc_of[r][:].bitcast(F32)[:, 256 * g + u : 256 * (g + 1) : 2],
+                        ident[:],
+                    )
+            halves = tw[:].bitcast(BF16).rearrange("p (u c e) -> p u c e", u=2, e=2)
+            for u in range(2):
+                for e in range(2):
+                    t = 2 * u + e
+                    nc.scalar.activation(
+                        out=planes[:, g, t, :],
+                        in_=halves[:, u, :, e],
+                        func=ACT.Copy,
+                        scale=scl_t[:, g, t : t + 1],
+                    )
+
+        def weave_x(gp):
+            gs = slice(2 * gp, 2 * gp + 2)
+            nc.scalar.copy(out=xg_view[:, gs, :, :], in_=planes[:, gs, :, :].rearrange("p g t c -> p g c t"))
+
+        def quant_x(gp):
+            nc.vector.quantize_mx(
+                out=xcodes[:, 2 * gp * XC : (2 * gp + 2) * XC].bitcast(FP8X4),
+                scales=xscales[:, 2 * gp * XC : (2 * gp + 2) * XC],
+                in_=xg[:, 2 * gp * XC * 4 : (2 * gp + 2) * XC * 4],
+            )
+
+        def live(h):
+            return 0 <= h < HR
+
+        def finish(h):
+            rope(h, 0, B)
+            turn_back(h, 0, B)
+
+        tables_raw()
+        for j in range(HR + 3):
+            rope_heads = [0, 1] if j == 4 else ([j - 3] if j >= 5 else [])
+            if live(j):
+                product(j)
+                turn_w(j, 0)
+                turn_w(j, 1)
+            if j == 0:
+                tables()
+            if j in (0, 1):
+                for b in range(B):
+                    turn_q(b, j)
+            if j == 2:
+                quant_q(0)
+                quant_q(1)
+            if j == 3:
+                quant_q(2)
+                quant_q(3)
+                multiply(0)
+                multiply(1)
+            if j in (3, 4):
+                widen(j - 3)
+            if 5 <= j < 9:
+                turn_x(j - 5)
+            for h in rope_heads:
+                if h == HR - 1:
+                    for b0, nb in ((0, 2), (2, 1), (3, 1)):
+                        rope(h, b0, nb)
+                        turn_back(h, b0, nb)
+                else:
+                    finish(h)
+            if j in (14, 15):
+                finish(HR + j - 14)
+            if j in (9, 10):
+                weave_x(j - 9)
+            if j in (11, 12):
+                quant_x(j - 11)
+            if live(j - 1):
+                quant_w(j - 1)
+                if j >= 3:
+                    multiply(j - 1)
+            if j in (12, 13):
+                multiply(HR + j - 12)

@@ -68,6 +68,10 @@ def tile_attention_pa_kernel(tc, query, wq_bytes, wq_scale, bq, cos, sin, out):
         scl_t = const.tile([P, G, 4], F32, name="scl_t")
         nc.scalar.dma_start(out=scl_t[:], in_=wq_scale.rearrange("o (g p t) -> p (o g) t", p=P, t=4))
 
+        one = const.tile([P, 1], F32, name="one")
+        nc.gpsimd.memset(one[:], 1.0)
+        first = const.tile([P, 1], F32, name="first")
+        nc.scalar.activation(out=first[:], in_=one[:], func=ACT.Copy, scale=1.0)
         ident = const.tile([P, P], F32, name="ident")
         make_identity(nc, ident[:])
         perm = const.tile([P, P], F32, name="perm")
@@ -114,7 +118,7 @@ def tile_attention_pa_kernel(tc, query, wq_bytes, wq_scale, bq, cos, sin, out):
         ot_of = {}
 
         def product(h):
-            wb_of[h] = work.tile([P, K], BF16, name="wb", tag="wb")
+            wb_of[h] = work.tile([P, K], BF16, name="wb", tag="wb", bufs=4)
             cuts = (0, 2048)
             for c0, c1 in zip(cuts[:-1], cuts[1:]):
                 nc.vector.tensor_tensor(
@@ -126,7 +130,7 @@ def tile_attention_pa_kernel(tc, query, wq_bytes, wq_scale, bq, cos, sin, out):
 
         def turn_w(h, gp):
             if gp == 0:
-                wg_of[h] = work.tile([P, K], BF16, name="wg", tag="wg", align_bytes=64)
+                wg_of[h] = work.tile([P, K], BF16, name="wg", tag="wg", align_bytes=64, bufs=4)
             wg_words = wg_of[h][:].bitcast(F32).rearrange("p (g r u) -> p g r u", g=G, u=2)
             src = transpose_pair(wb_of[h][:].bitcast(F32), gp)
             nc.scalar.copy(out=wg_words[:, 2 * gp : 2 * gp + 2, :, :], in_=src)
@@ -173,8 +177,8 @@ def tile_attention_pa_kernel(tc, query, wq_bytes, wq_scale, bq, cos, sin, out):
 
         def rope(h, b0, nb):
             cs = slice(b0 * P, (b0 + nb) * P)
-            uu = work.tile([P, nb * P], F32, name="uu", tag="uu")
-            ww = work.tile([P, nb * P], F32, name="ww", tag="ww")
+            uu = work.tile([P, nb * P], F32, name="uu", tag="uu", bufs=4)
+            ww = work.tile([P, nb * P], F32, name="ww", tag="ww", bufs=4)
             for dst, a in ((uu, 0), (ww, 1)):
                 nc.vector.scalar_tensor_tensor(
                     out=dst[:].rearrange("p (b s) -> p b s", b=nb),
@@ -197,7 +201,7 @@ def tile_attention_pa_kernel(tc, query, wq_bytes, wq_scale, bq, cos, sin, out):
                 nc.tensor.matmul(
                     out=ot[:, cs], lhsT=ww[:, cs], rhs=perm[:], is_transpose=True, start=False, stop=True
                 )
-            osb = work.tile([P, nb * P], F32, name="osb", tag="osb", bufs=6)
+            osb = work.tile([P, nb * P], F32, name="osb", tag="osb", bufs=8)
             nc.scalar.copy(out=osb[:], in_=ot[:])
             nc.sync.dma_start(
                 out=out[b0 : b0 + nb, h, :, :].rearrange("b s d -> s b d"),
@@ -261,11 +265,11 @@ def tile_attention_pa_kernel(tc, query, wq_bytes, wq_scale, bq, cos, sin, out):
                 product(j)
                 turn_w(j, 0)
                 turn_w(j, 1)
-            if j == 0:
-                tables()
             if j in (0, 1):
                 for b in range(B):
                     turn_q(b, j)
+            if j == 2:
+                tables()
             if j == 2:
                 quant_q(0)
                 quant_q(1)

@@ -190,9 +190,12 @@ def tile_attention_pa_kernel(tc, query, wq_bytes, wq_scale, bq, cos, sin, out):
                 )
             uw_of[(h, b0)] = (uu, ww)
 
-        def turn_back(h, b0, nb):
+        def turn_back(h, b0, nb, late=False):
             uu, ww = uw_of[(h, b0)]
-            ot = psum.tile([P, nb * P], F32, name="ot", tag="ot", bufs=2)
+            if late:
+                ot = psum.tile([P, nb * P], F32, name="ot", tag="tw", bufs=3)
+            else:
+                ot = psum.tile([P, nb * P], F32, name="ot", tag="ot", bufs=2)
             for b in range(nb):
                 cs = slice(b * P, (b + 1) * P)
                 nc.tensor.matmul(
@@ -254,9 +257,9 @@ def tile_attention_pa_kernel(tc, query, wq_bytes, wq_scale, bq, cos, sin, out):
         def live(h):
             return 0 <= h < HR
 
-        def finish(h):
+        def finish(h, late=False):
             rope(h, 0, B)
-            turn_back(h, 0, B)
+            turn_back(h, 0, B, late)
 
         tables_raw()
         for j in range(HR + 3):
@@ -286,11 +289,11 @@ def tile_attention_pa_kernel(tc, query, wq_bytes, wq_scale, bq, cos, sin, out):
                 if h == HR - 1:
                     for b0, nb in ((0, 2), (2, 1), (3, 1)):
                         rope(h, b0, nb)
-                        turn_back(h, b0, nb)
+                        turn_back(h, b0, nb, b0 != 2)
                 else:
                     finish(h)
             if j in (14, 15):
-                finish(HR + j - 14)
+                finish(HR + j - 14, True)
             if j in (9, 10):
                 weave_x(j - 9)
             if j in (11, 12):

@@ -37,10 +37,22 @@ def tile_attention_pa_kernel(tc, query, wq_bytes, wq_scale, bq, cos, sin, out):
         scl = const.tile([P, K], F32, name="scl")
         xq = const.tile([P, B, K], BF16, name="xq")
         craw = const.tile([P, 3, P], BF16, name="craw")
-        scale_row = wq_scale.rearrange("o k -> (o k)")
+        scl_t = const.tile([P, G, 8], F32, name="scl_t")
+        for g in range(G):
+            nc.scalar.dma_start(
+                out=scl_t[:, g, 0:4], in_=wq_scale.rearrange("o (g p t) -> g p (o t)", p=P, t=4)[g]
+            )
 
-        def load_scl(c0, c1):
-            nc.scalar.dma_start(out=scl[:, c0:c1], in_=scale_row[c0:c1].partition_broadcast(P))
+        one = const.tile([P, 1], F32, name="one")
+        nc.vector.memset(one[:], 1.0)
+        first = const.tile([P, 1], F32, name="first")
+        nc.scalar.activation(out=first[:], in_=one[:], func=ACT.Copy, scale=1.0)
+        ident = const.tile([P, P], F32, name="ident")
+        make_identity(nc, ident[:])
+        nc.gpsimd.memset(craw[:, 2, :], 0.0)
+        perm = const.tile([P, P], F32, name="perm")
+        nc.gpsimd.tensor_copy(out=perm[:, 0:64], in_=ident[:, 64:128])
+        nc.gpsimd.tensor_copy(out=perm[:, 64:128], in_=ident[:, 0:64])
 
         def load_w(h, c0=0, c1=K):
             nc.sync.dma_start(out=wq_bytes_sb[:, h, c0:c1], in_=wq_bytes[h * P : (h + 1) * P, c0:c1])
@@ -49,7 +61,6 @@ def tile_attention_pa_kernel(tc, query, wq_bytes, wq_scale, bq, cos, sin, out):
             cs = slice(gp * 1024, (gp + 1) * 1024)
             nc.sync.dma_start(out=xq[:, b, cs], in_=query[b, :, cs])
 
-        load_scl(0, K)
         load_w(0)
         load_w(1)
         for b in range(B):
@@ -57,26 +68,26 @@ def tile_attention_pa_kernel(tc, query, wq_bytes, wq_scale, bq, cos, sin, out):
         load_w(2)
         for b in range(B):
             load_q(b, 1)
-        for h in (3, 4, HR, HR + 1):
+        load_w(3)
+        nc.sync.dma_start(out=craw[:, 0, :], in_=cos[0, 0])
+        nc.sync.dma_start(out=craw[:, 1, :], in_=sin[0, 0])
+        nc.sync.dma_start(out=craw[0:H, 2, :], in_=bq.rearrange("(h d) -> h d", d=P))
+        for h in (4, HR, HR + 1):
             load_w(h)
         for h in range(5, HR):
             load_w(h)
-        nc.gpsimd.memset(craw[:, 2, :], 0.0)
-        nc.scalar.dma_start(out=craw[:, 0, :], in_=cos[0, 0])
-        nc.scalar.dma_start(out=craw[:, 1, :], in_=sin[0, 0])
-        nc.scalar.dma_start(out=craw[0:H, 2, :], in_=bq.rearrange("(h d) -> h d", d=P))
-        scl_t = const.tile([P, G, 4], F32, name="scl_t")
-        nc.scalar.dma_start(out=scl_t[:], in_=wq_scale.rearrange("o (g p t) -> p (o g) t", p=P, t=4))
 
-        one = const.tile([P, 1], F32, name="one")
-        nc.gpsimd.memset(one[:], 1.0)
-        first = const.tile([P, 1], F32, name="first")
-        nc.scalar.activation(out=first[:], in_=one[:], func=ACT.Copy, scale=1.0)
-        ident = const.tile([P, P], F32, name="ident")
-        make_identity(nc, ident[:])
-        perm = const.tile([P, P], F32, name="perm")
-        nc.gpsimd.tensor_copy(out=perm[:, 0:64], in_=ident[:, 64:128])
-        nc.gpsimd.tensor_copy(out=perm[:, 64:128], in_=ident[:, 0:64])
+        def spread_scales():
+            for g in range(G):
+                spread = psum.tile([P, 512], F32, name="spread", tag="tw", bufs=3)
+                for t in range(4):
+                    column = scl_t[:, g, t : t + 1]
+                    nc.tensor.transpose(spread[:, t * P : (t + 1) * P], column.to_broadcast([P, P]), ident[:])
+                nc.scalar.copy(
+                    out=scl[:, g * 512 : (g + 1) * 512].rearrange("p (c t) -> p c t", t=4),
+                    in_=spread[:].rearrange("p (t c) -> p c t", t=4),
+                )
+
         stg = const.tile([P, 3, P], F32, name="stg")
         tab = const.tile([P, 3, P], F32, name="tab")
 
@@ -119,7 +130,7 @@ def tile_attention_pa_kernel(tc, query, wq_bytes, wq_scale, bq, cos, sin, out):
 
         def product(h):
             wb_of[h] = work.tile([P, K], BF16, name="wb", tag="wb", bufs=4)
-            cuts = (0, 2048)
+            cuts = (0, 512, 1024, 1536, 2048) if h == 0 else (0, 2048)
             for c0, c1 in zip(cuts[:-1], cuts[1:]):
                 nc.vector.tensor_tensor(
                     out=wb_of[h][:, c0:c1],
@@ -261,7 +272,7 @@ def tile_attention_pa_kernel(tc, query, wq_bytes, wq_scale, bq, cos, sin, out):
             rope(h, 0, B)
             turn_back(h, 0, B, late)
 
-        tables_raw()
+        spread_scales()
         for j in range(HR + 3):
             rope_heads = [0, 1] if j == 4 else ([j - 3] if j >= 5 else [])
             if live(j):
@@ -272,6 +283,7 @@ def tile_attention_pa_kernel(tc, query, wq_bytes, wq_scale, bq, cos, sin, out):
                 for b in range(B):
                     turn_q(b, j)
             if j == 2:
+                tables_raw()
                 tables()
             if j == 2:
                 quant_q(0)

@@ -20,8 +20,8 @@ H = 16
 K = 2048
 G = 4
 TOK = 512
-HR = 14
-NX = 2
+HR = 13
+NX = 3
 
 
 def tile_attention_pa_kernel(tc, query, wq_bytes, wq_scale, bq, cos, sin, out):
@@ -61,6 +61,8 @@ def tile_attention_pa_kernel(tc, query, wq_bytes, wq_scale, bq, cos, sin, out):
             cs = slice(gp * 1024, (gp + 1) * 1024)
             nc.sync.dma_start(out=xq[:, b, cs], in_=query[b, :, cs])
 
+        load_w(HR)
+        load_w(HR + 1)
         load_w(0)
         load_w(1)
         for b in range(B):
@@ -72,7 +74,7 @@ def tile_attention_pa_kernel(tc, query, wq_bytes, wq_scale, bq, cos, sin, out):
         nc.sync.dma_start(out=craw[:, 0, :], in_=cos[0, 0])
         nc.sync.dma_start(out=craw[:, 1, :], in_=sin[0, 0])
         nc.sync.dma_start(out=craw[0:H, 2, :], in_=bq.rearrange("(h d) -> h d", d=P))
-        for h in (4, HR, HR + 1):
+        for h in (4, HR + 2):
             load_w(h)
         for h in range(5, HR):
             load_w(h)
@@ -106,8 +108,8 @@ def tile_attention_pa_kernel(tc, query, wq_bytes, wq_scale, bq, cos, sin, out):
         qg = const.tile([P, G * TOK * 4], BF16, name="qg", align_bytes=64)
         qcodes = const.tile([P, G * TOK], U32, name="qcodes", align_bytes=64)
         qscales = const.tile([P, G * TOK], U8, name="qscales", align_bytes=64)
-        wcodes = const.tile([P, HR, G * P], U32, name="wcodes", align_bytes=64)
-        wscales = const.tile([P, HR, G * P], U8, name="wscales", align_bytes=64)
+        wcodes = const.tile([P, H, G * P], U32, name="wcodes", align_bytes=64)
+        wscales = const.tile([P, H, G * P], U8, name="wscales", align_bytes=64)
         qg_words = qg[:].bitcast(F32).rearrange("p (g n u) -> p g n u", g=G, n=TOK, u=2)
 
         def transpose_pair(words, gp):
@@ -159,27 +161,21 @@ def tile_attention_pa_kernel(tc, query, wq_bytes, wq_scale, bq, cos, sin, out):
 
         def quant_w(h):
             nc.vector.quantize_mx(
-                out=wcodes[:, h, :].bitcast(FP8X4), scales=wscales[:, h, :], in_=wg_of[h][:]
+                out=wcodes[:, h, :].bitcast(FP8X4),
+                scales=wscales[:, h, :],
+                in_=wg_of[h][:] if h < HR else xg[:, h - HR, :],
             )
 
-        def codes_of(h, g):
-            if h < HR:
-                return wcodes[:, h, g * P : (g + 1) * P]
-            return xcodes[:, g * NX * P + (h - HR) * P : g * NX * P + (h - HR + 1) * P]
-
-        def scales_of(h, g):
-            if h < HR:
-                return wscales[:, h, g * P : (g + 1) * P]
-            return xscales[:, g * NX * P + (h - HR) * P : g * NX * P + (h - HR + 1) * P]
-
-        def multiply(h, passes=(0, 1, 2, 3)):
-            if passes[0] == 0:
+        def multiply(h, late=False):
+            if late:
+                acc_of[h] = psum.tile([P, TOK], F32, name="acc", tag="tw", bufs=3)
+            else:
                 acc_of[h] = psum.tile([P, TOK], F32, name="acc", tag="acc", bufs=3)
-            for g in passes:
+            for g in range(G):
                 nc.tensor.matmul_mx(
                     out=acc_of[h][:],
-                    lhsT=codes_of(h, g).bitcast(FP8X4),
-                    lhsT_scale=scales_of(h, g),
+                    lhsT=wcodes[:, h, g * P : (g + 1) * P].bitcast(FP8X4),
+                    lhsT_scale=wscales[:, h, g * P : (g + 1) * P],
                     rhs=qcodes[:, g * TOK : (g + 1) * TOK].bitcast(FP8X4),
                     rhs_scale=qscales[:, g * TOK : (g + 1) * TOK],
                     start=(g == 0),
@@ -224,45 +220,41 @@ def tile_attention_pa_kernel(tc, query, wq_bytes, wq_scale, bq, cos, sin, out):
 
         XC = NX * P
         planes = const.tile([P, G, 4, XC], BF16, name="planes")
-        xg = const.tile([P, G * XC * 4], BF16, name="xg", align_bytes=64)
-        xcodes = const.tile([P, G * XC], U32, name="xcodes", align_bytes=64)
-        xscales = const.tile([P, G * XC], U8, name="xscales", align_bytes=64)
-        xg_view = xg[:].rearrange("p (g c t) -> p g c t", g=G, t=4)
+        xg = const.tile([P, NX, K], BF16, name="xg", align_bytes=64)
+        xg_view = xg[:].rearrange("p r (g c t) -> p r g c t", g=G, t=4)
         wc_of = {}
 
-        def widen(r):
+        def widen(r, on_vector):
             wc_of[r] = const.tile([P, K], BF16, name="wc%d" % r)
-            nc.scalar.copy(out=wc_of[r][:], in_=wq_bytes_sb[:, HR + r, :].bitcast(FP8))
+            src = wq_bytes_sb[:, HR + r, :].bitcast(FP8)
+            if on_vector:
+                nc.vector.tensor_copy(out=wc_of[r][:], in_=src)
+            else:
+                nc.scalar.copy(out=wc_of[r][:], in_=src)
 
         def turn_x(g):
-            tw = psum.tile([P, 512], F32, name="tw", tag="tw", bufs=3)
             for u in range(2):
+                tw = psum.tile([P, 512], F32, name="tw", tag="tw", bufs=3)
                 for r in range(NX):
                     nc.tensor.transpose(
-                        tw[:, (u * NX + r) * P : (u * NX + r + 1) * P],
+                        tw[:, r * P : (r + 1) * P],
                         wc_of[r][:].bitcast(F32)[:, 256 * g + u : 256 * (g + 1) : 2],
                         ident[:],
                     )
-            halves = tw[:].bitcast(BF16).rearrange("p (u c e) -> p u c e", u=2, e=2)
-            for u in range(2):
+                pairs = tw[:].bitcast(BF16).rearrange("p (c e) -> p c e", e=2)
                 for e in range(2):
                     t = 2 * u + e
                     nc.scalar.activation(
                         out=planes[:, g, t, :],
-                        in_=halves[:, u, :, e],
+                        in_=pairs[:, 0:XC, e],
                         func=ACT.Copy,
                         scale=scl_t[:, g, t : t + 1],
                     )
 
-        def weave_x(gp):
-            gs = slice(2 * gp, 2 * gp + 2)
-            nc.scalar.copy(out=xg_view[:, gs, :, :], in_=planes[:, gs, :, :].rearrange("p g t c -> p g c t"))
-
-        def quant_x(gp):
-            nc.vector.quantize_mx(
-                out=xcodes[:, 2 * gp * XC : (2 * gp + 2) * XC].bitcast(FP8X4),
-                scales=xscales[:, 2 * gp * XC : (2 * gp + 2) * XC],
-                in_=xg[:, 2 * gp * XC * 4 : (2 * gp + 2) * XC * 4],
+        def weave_x(g):
+            nc.scalar.copy(
+                out=xg_view[:, :, g, :, :],
+                in_=planes[:, g, :, :].rearrange("p t (r c) -> p r c t", r=NX),
             )
 
         def live(h):
@@ -272,6 +264,8 @@ def tile_attention_pa_kernel(tc, query, wq_bytes, wq_scale, bq, cos, sin, out):
             rope(h, 0, B)
             turn_back(h, 0, B, late)
 
+        widen(0, True)
+        widen(1, True)
         spread_scales()
         for j in range(HR + 3):
             rope_heads = [0, 1] if j == 4 else ([j - 3] if j >= 5 else [])
@@ -293,26 +287,29 @@ def tile_attention_pa_kernel(tc, query, wq_bytes, wq_scale, bq, cos, sin, out):
                 quant_q(3)
                 multiply(0)
                 multiply(1)
-            if j in (3, 4):
-                widen(j - 3)
-            if 5 <= j < 9:
-                turn_x(j - 5)
             for h in rope_heads:
-                if h == HR - 1:
-                    for b0, nb in ((0, 2), (2, 1), (3, 1)):
-                        rope(h, b0, nb)
-                        turn_back(h, b0, nb, b0 != 2)
-                else:
-                    finish(h)
-            if j in (14, 15):
-                finish(HR + j - 14, True)
-            if j in (9, 10):
-                weave_x(j - 9)
-            if j in (11, 12):
-                quant_x(j - 11)
+                finish(h)
+            if j == HR:
+                finish(HR, True)
+            if j == HR + 1:
+                finish(HR + 1, True)
             if live(j - 1):
                 quant_w(j - 1)
+                if j == HR:
+                    multiply(HR + 1)
+                    multiply(HR + 2, True)
                 if j >= 3:
                     multiply(j - 1)
-            if j in (12, 13):
-                multiply(HR + j - 12)
+            if j == HR - 1:
+                for r in range(NX):
+                    quant_w(HR + r)
+                multiply(HR)
+            if j == 3:
+                widen(2, False)
+            if 4 <= j < 8:
+                turn_x(j - 4)
+            if 8 <= j < 12:
+                weave_x(j - 8)
+        for b0, nb in ((0, 2), (2, 1), (3, 1)):
+            rope(HR + 2, b0, nb)
+            turn_back(HR + 2, b0, nb, b0 != 2)

@@ -130,9 +130,11 @@ def tile_attention_pa_kernel(tc, query, wq_bytes, wq_scale, bq, cos, sin, out):
         uw_of = {}
         ot_of = {}
 
-        def product(h):
-            wb_of[h] = work.tile([P, K], BF16, name="wb", tag="wb", bufs=4)
-            cuts = (0, 512, 1024, 1536, 2048) if h == 0 else (0, 2048)
+        def product(h, gp):
+            if gp == 0:
+                wb_of[h] = work.tile([P, K], BF16, name="wb", tag="wb", bufs=4)
+            k0 = 1024 * gp
+            cuts = (k0, k0 + 512, k0 + 1024) if h == 0 else (k0, k0 + 1024)
             for c0, c1 in zip(cuts[:-1], cuts[1:]):
                 nc.vector.tensor_tensor(
                     out=wb_of[h][:, c0:c1],
@@ -166,12 +168,10 @@ def tile_attention_pa_kernel(tc, query, wq_bytes, wq_scale, bq, cos, sin, out):
                 in_=wg_of[h][:] if h < HR else xg[:, h - HR, :],
             )
 
-        def multiply(h, late=False):
-            if late:
-                acc_of[h] = psum.tile([P, TOK], F32, name="acc", tag="tw", bufs=3)
-            else:
+        def multiply(h, passes=(0, 1, 2, 3)):
+            if passes[0] == 0:
                 acc_of[h] = psum.tile([P, TOK], F32, name="acc", tag="acc", bufs=3)
-            for g in range(G):
+            for g in passes:
                 nc.tensor.matmul_mx(
                     out=acc_of[h][:],
                     lhsT=wcodes[:, h, g * P : (g + 1) * P].bitcast(FP8X4),
@@ -218,10 +218,10 @@ def tile_attention_pa_kernel(tc, query, wq_bytes, wq_scale, bq, cos, sin, out):
                 in_=osb[:].rearrange("p (b d) -> p b d", b=nb),
             )
 
-        XC = NX * P
-        planes = const.tile([P, G, 4, XC], BF16, name="planes")
         xg = const.tile([P, NX, K], BF16, name="xg", align_bytes=64)
         xg_view = xg[:].rearrange("p r (g c t) -> p r g c t", g=G, t=4)
+        early = const.tile([P, G, 4, 2 * P], BF16, name="early")
+        single = const.tile([P, G, 4, P], BF16, name="single")
         wc_of = {}
 
         def widen(r, on_vector):
@@ -232,30 +232,51 @@ def tile_attention_pa_kernel(tc, query, wq_bytes, wq_scale, bq, cos, sin, out):
             else:
                 nc.scalar.copy(out=wc_of[r][:], in_=src)
 
-        def turn_x(g):
-            for u in range(2):
-                tw = psum.tile([P, 512], F32, name="tw", tag="tw", bufs=3)
-                for r in range(NX):
-                    nc.tensor.transpose(
-                        tw[:, r * P : (r + 1) * P],
-                        wc_of[r][:].bitcast(F32)[:, 256 * g + u : 256 * (g + 1) : 2],
-                        ident[:],
-                    )
-                pairs = tw[:].bitcast(BF16).rearrange("p (c e) -> p c e", e=2)
-                for e in range(2):
-                    t = 2 * u + e
+        def turn_x(dst, pieces, width):
+            tw = psum.tile([P, 512], F32, name="tw", tag="tw", bufs=3)
+            col = 0
+            for g, heads in pieces:
+                for u in range(2):
+                    for r in heads:
+                        nc.tensor.transpose(
+                            tw[:, col : col + P],
+                            wc_of[r][:].bitcast(F32)[:, 256 * g + u : 256 * (g + 1) : 2],
+                            ident[:],
+                        )
+                        col += P
+            pairs = tw[:].bitcast(BF16).rearrange("p (q c e) -> p q c e", c=width, e=2)
+            for i, (g, heads) in enumerate(pieces):
+                for t in range(4):
                     nc.scalar.activation(
-                        out=planes[:, g, t, :],
-                        in_=pairs[:, 0:XC, e],
+                        out=dst[:, g, t, :],
+                        in_=pairs[:, 2 * i + t // 2, :, t % 2],
                         func=ACT.Copy,
                         scale=scl_t[:, g, t : t + 1],
                     )
 
-        def weave_x(g):
+        def weave_early(g):
             nc.scalar.copy(
-                out=xg_view[:, :, g, :, :],
-                in_=planes[:, g, :, :].rearrange("p t (r c) -> p r c t", r=NX),
+                out=xg_view[:, 0:2, g, :, :],
+                in_=early[:, g, :, :].rearrange("p t (r c) -> p r c t", r=2),
             )
+
+        def weave_single():
+            nc.scalar.copy(out=xg_view[:, 2, :, :, :], in_=single[:].rearrange("p g t c -> p g c t"))
+
+        def road(j):
+            if 3 <= j < 7:
+                turn_x(early, [(j - 3, (0, 1))], 2 * P)
+            if j in (5, 6):
+                weave_early(j - 5)
+            if j == 7:
+                weave_early(2)
+                weave_early(3)
+            if j == 8:
+                widen(2, False)
+            if j in (9, 10):
+                turn_x(single, [(2 * j - 18, (2,)), (2 * j - 17, (2,))], P)
+            if j == 11:
+                weave_single()
 
         def live(h):
             return 0 <= h < HR
@@ -270,8 +291,12 @@ def tile_attention_pa_kernel(tc, query, wq_bytes, wq_scale, bq, cos, sin, out):
         for j in range(HR + 3):
             rope_heads = [0, 1] if j == 4 else ([j - 3] if j >= 5 else [])
             if live(j):
-                product(j)
+                product(j, 0)
                 turn_w(j, 0)
+            if j >= 4 and live(j - 2) and j - 2 != HR - 1:
+                multiply(j - 2, (2, 3))
+            if live(j):
+                product(j, 1)
                 turn_w(j, 1)
             if j in (0, 1):
                 for b in range(B):
@@ -288,28 +313,24 @@ def tile_attention_pa_kernel(tc, query, wq_bytes, wq_scale, bq, cos, sin, out):
                 multiply(0)
                 multiply(1)
             for h in rope_heads:
-                finish(h)
-            if j == HR:
-                finish(HR, True)
+                if h < HR - 1:
+                    finish(h)
+                else:
+                    for b0, nb in ((0, 2), (2, 1), (3, 1)):
+                        rope(h, b0, nb)
+                        turn_back(h, b0, nb, b0 != 2)
+            if j in (9, 10):
+                finish(HR + j - 9)
             if j == HR + 1:
-                finish(HR + 1, True)
+                finish(HR + 2, True)
             if live(j - 1):
                 quant_w(j - 1)
                 if j == HR:
-                    multiply(HR + 1)
-                    multiply(HR + 2, True)
-                if j >= 3:
                     multiply(j - 1)
-            if j == HR - 1:
-                for r in range(NX):
-                    quant_w(HR + r)
-                multiply(HR)
-            if j == 3:
-                widen(2, False)
-            if 4 <= j < 8:
-                turn_x(j - 4)
-            if 8 <= j < 12:
-                weave_x(j - 8)
-        for b0, nb in ((0, 2), (2, 1), (3, 1)):
-            rope(HR + 2, b0, nb)
-            turn_back(HR + 2, b0, nb, b0 != 2)
+                elif j >= 3:
+                    multiply(j - 1, (0, 1))
+            if j in (8, 9, HR - 1):
+                h = HR + {8: 0, 9: 1, HR - 1: 2}[j]
+                quant_w(h)
+                multiply(h)
+            road(j)

@@ -165,17 +165,30 @@ def tile_attention_pa_kernel(tc, query, wq_bytes, wq_scale, bq, cos, sin, out):
             nc.vector.quantize_mx(
                 out=wcodes[:, h, :].bitcast(FP8X4),
                 scales=wscales[:, h, :],
-                in_=wg_of[h][:] if h < HR else xg[:, h - HR, :],
+                in_=wg_of[h][:] if h < HR else xsingle[:],
+            )
+
+        def quant_early(gp):
+            nc.vector.quantize_mx(
+                out=xcodes[:, gp * 512 : (gp + 1) * 512].bitcast(FP8X4),
+                scales=xscales[:, gp * 512 : (gp + 1) * 512],
+                in_=xearly[:, gp * 2048 : (gp + 1) * 2048],
             )
 
         def multiply(h, passes=(0, 1, 2, 3)):
             if passes[0] == 0:
                 acc_of[h] = psum.tile([P, TOK], F32, name="acc", tag="acc", bufs=3)
             for g in passes:
+                if h in (HR, HR + 1):
+                    cols = slice((2 * g + h - HR) * P, (2 * g + h - HR + 1) * P)
+                    codes, scales = xcodes[:, cols], xscales[:, cols]
+                else:
+                    cols = slice(g * P, (g + 1) * P)
+                    codes, scales = wcodes[:, h, cols], wscales[:, h, cols]
                 nc.tensor.matmul_mx(
                     out=acc_of[h][:],
-                    lhsT=wcodes[:, h, g * P : (g + 1) * P].bitcast(FP8X4),
-                    lhsT_scale=wscales[:, h, g * P : (g + 1) * P],
+                    lhsT=codes.bitcast(FP8X4),
+                    lhsT_scale=scales,
                     rhs=qcodes[:, g * TOK : (g + 1) * TOK].bitcast(FP8X4),
                     rhs_scale=qscales[:, g * TOK : (g + 1) * TOK],
                     start=(g == 0),
@@ -218,8 +231,10 @@ def tile_attention_pa_kernel(tc, query, wq_bytes, wq_scale, bq, cos, sin, out):
                 in_=osb[:].rearrange("p (b d) -> p b d", b=nb),
             )
 
-        xg = const.tile([P, NX, K], BF16, name="xg", align_bytes=64)
-        xg_view = xg[:].rearrange("p r (g c t) -> p r g c t", g=G, t=4)
+        xearly = const.tile([P, G * 2 * P * 4], BF16, name="xearly", align_bytes=64)
+        xsingle = const.tile([P, K], BF16, name="xsingle", align_bytes=64)
+        xcodes = const.tile([P, G * 2 * P], U32, name="xcodes", align_bytes=64)
+        xscales = const.tile([P, G * 2 * P], U8, name="xscales", align_bytes=64)
         early = const.tile([P, G, 4, 2 * P], BF16, name="early")
         single = const.tile([P, G, 4, P], BF16, name="single")
         wc_of = {}
@@ -256,12 +271,15 @@ def tile_attention_pa_kernel(tc, query, wq_bytes, wq_scale, bq, cos, sin, out):
 
         def weave_early(g):
             nc.scalar.copy(
-                out=xg_view[:, 0:2, g, :, :],
-                in_=early[:, g, :, :].rearrange("p t (r c) -> p r c t", r=2),
+                out=xearly[:, g * 1024 : (g + 1) * 1024].rearrange("p (c i t) -> p c t i", i=4, t=4),
+                in_=early[:, g, :, :].rearrange("p t (c i) -> p c t i", i=4),
             )
 
-        def weave_single():
-            nc.scalar.copy(out=xg_view[:, 2, :, :, :], in_=single[:].rearrange("p g t c -> p g c t"))
+        def weave_single(g):
+            nc.scalar.copy(
+                out=xsingle[:, g * 512 : (g + 1) * 512].rearrange("p (c i t) -> p c t i", i=4, t=4),
+                in_=single[:, g, :, :].rearrange("p t (c i) -> p c t i", i=4),
+            )
 
         def road(j):
             if 3 <= j < 7:
@@ -276,7 +294,8 @@ def tile_attention_pa_kernel(tc, query, wq_bytes, wq_scale, bq, cos, sin, out):
             if j in (9, 10):
                 turn_x(single, [(2 * j - 18, (2,)), (2 * j - 17, (2,))], P)
             if j == 11:
-                weave_single()
+                for g in range(G):
+                    weave_single(g)
 
         def live(h):
             return 0 <= h < HR
@@ -329,8 +348,11 @@ def tile_attention_pa_kernel(tc, query, wq_bytes, wq_scale, bq, cos, sin, out):
                     multiply(j - 1)
                 elif j >= 3:
                     multiply(j - 1, (0, 1))
+            if j == 8:
+                quant_early(0)
+                quant_early(1)
+            if j == HR - 1:
+                quant_w(HR + 2)
             if j in (8, 9, HR - 1):
-                h = HR + {8: 0, 9: 1, HR - 1: 2}[j]
-                quant_w(h)
-                multiply(h)
+                multiply(HR + {8: 0, 9: 1, HR - 1: 2}[j])
             road(j)

@@ -62,14 +62,15 @@ def tile_attention_pa_kernel(tc, query, wq_bytes, wq_scale, bq, cos, sin, out):
             nc.sync.dma_start(out=xq[:, b, cs], in_=query[b, :, cs])
 
         load_w(HR)
-        load_w(HR + 1)
+        load_q(0, 0)
         load_w(0)
-        load_w(1)
-        for b in range(B):
+        for b in range(1, B):
             load_q(b, 0)
-        load_w(2)
+        load_w(1)
+        load_w(HR + 1)
         for b in range(B):
             load_q(b, 1)
+        load_w(2)
         load_w(3)
         nc.sync.dma_start(out=craw[:, 0, :], in_=cos[0, 0])
         nc.sync.dma_start(out=craw[:, 1, :], in_=sin[0, 0])
@@ -305,49 +306,56 @@ def tile_attention_pa_kernel(tc, query, wq_bytes, wq_scale, bq, cos, sin, out):
             turn_back(h, 0, B, late)
 
         widen(0, True)
-        widen(1, True)
         spread_scales()
+        for b in range(B):
+            turn_q(b, 0)
         for j in range(HR + 3):
-            rope_heads = [0, 1] if j == 4 else ([j - 3] if j >= 5 else [])
             if live(j):
                 product(j, 0)
                 turn_w(j, 0)
+            if j == 2:
+                turn_q(2, 1)
+                turn_q(3, 1)
+            if j == 4:
+                multiply(1, (2, 3))
             if j >= 4 and live(j - 2) and j - 2 != HR - 1:
                 multiply(j - 2, (2, 3))
             if live(j):
                 product(j, 1)
                 turn_w(j, 1)
-            if j in (0, 1):
-                for b in range(B):
-                    turn_q(b, j)
-            if j == 2:
-                tables_raw()
-                tables()
-            if j == 2:
-                quant_q(0)
-                quant_q(1)
-            if j == 3:
-                quant_q(2)
-                quant_q(3)
-                multiply(0)
-                multiply(1)
-            for h in rope_heads:
-                if h < HR - 1:
-                    finish(h)
-                else:
-                    for b0, nb in ((0, 2), (2, 1), (3, 1)):
-                        rope(h, b0, nb)
-                        turn_back(h, b0, nb, b0 != 2)
+            if j == 4:
+                finish(0)
+            elif j == 5:
+                finish(1)
+                finish(2)
+            elif 6 <= j < HR + 2:
+                finish(j - 3)
+            elif j == HR + 2:
+                for b0, nb in ((0, 2), (2, 1), (3, 1)):
+                    rope(j - 3, b0, nb)
+                    turn_back(j - 3, b0, nb, b0 != 2)
             if j in (9, 10):
                 finish(HR + j - 9)
             if j == HR + 1:
                 finish(HR + 2, True)
+            if j in (1, 3):
+                quant_q(j - 1)
+                quant_q(j)
+            if j == 3:
+                multiply(0, (2, 3))
             if live(j - 1):
                 quant_w(j - 1)
                 if j == HR:
                     multiply(j - 1)
-                elif j >= 3:
+                else:
                     multiply(j - 1, (0, 1))
+            if j == 1:
+                turn_q(0, 1)
+                turn_q(1, 1)
+                widen(1, True)
+            if j == 2:
+                tables_raw()
+                tables()
             if j == 8:
                 quant_early(0)
                 quant_early(1)

@@ -155,11 +155,12 @@ def tile_attention_pa_kernel(tc, query, wq_bytes, wq_scale, bq, cos, sin, out):
             src = transpose_pair(xq[:, b, :].bitcast(F32), gp)
             nc.scalar.copy(out=qg_words[:, 2 * gp : 2 * gp + 2, b * P : (b + 1) * P, :], in_=src)
 
-        def quant_q(g):
+        def quant_q(gp):
+            cols = slice(2 * gp * TOK, (2 * gp + 2) * TOK)
             nc.vector.quantize_mx(
-                out=qcodes[:, g * TOK : (g + 1) * TOK].bitcast(FP8X4),
-                scales=qscales[:, g * TOK : (g + 1) * TOK],
-                in_=qg[:, g * TOK * 4 : (g + 1) * TOK * 4],
+                out=qcodes[:, cols].bitcast(FP8X4),
+                scales=qscales[:, cols],
+                in_=qg[:, 2 * gp * TOK * 4 : (2 * gp + 2) * TOK * 4],
             )
 
         def quant_w(h):
@@ -283,18 +284,17 @@ def tile_attention_pa_kernel(tc, query, wq_bytes, wq_scale, bq, cos, sin, out):
             )
 
         def road(j):
-            if 3 <= j < 7:
-                turn_x(early, [(j - 3, (0, 1))], 2 * P)
-            if j in (5, 6):
-                weave_early(j - 5)
-            if j == 7:
-                weave_early(2)
+            if 2 <= j < 6:
+                turn_x(early, [(j - 2, (0, 1))], 2 * P)
+            if 4 <= j < 7:
+                weave_early(j - 4)
+            if j == 6:
                 weave_early(3)
-            if j == 8:
+            if j == 7:
                 widen(2, False)
-            if j in (9, 10):
-                turn_x(single, [(2 * j - 18, (2,)), (2 * j - 17, (2,))], P)
-            if j == 11:
+            if j in (8, 9):
+                turn_x(single, [(2 * j - 16, (2,)), (2 * j - 15, (2,))], P)
+            if j == 10:
                 for g in range(G):
                     weave_single(g)
 
@@ -339,8 +339,7 @@ def tile_attention_pa_kernel(tc, query, wq_bytes, wq_scale, bq, cos, sin, out):
             if j == HR + 1:
                 finish(HR + 2, True)
             if j in (1, 3):
-                quant_q(j - 1)
-                quant_q(j)
+                quant_q(j // 2)
             if j == 3:
                 multiply(0, (2, 3))
             if live(j - 1):
@@ -359,8 +358,8 @@ def tile_attention_pa_kernel(tc, query, wq_bytes, wq_scale, bq, cos, sin, out):
             if j == 8:
                 quant_early(0)
                 quant_early(1)
-            if j == HR - 1:
+            if j == 11:
                 quant_w(HR + 2)
-            if j in (8, 9, HR - 1):
-                multiply(HR + {8: 0, 9: 1, HR - 1: 2}[j])
+            if j in (8, 9, 11):
+                multiply(HR + {8: 0, 9: 1, 11: 2}[j])
             road(j)

from contextlib import ExitStack

import concourse.mybir as mybir
from concourse.masks import make_identity

FLOPS = 2 * 512 * 2048 * 2048

F32 = mybir.dt.float32
BF16 = mybir.dt.bfloat16
U32 = mybir.dt.uint32
U8 = mybir.dt.uint8
FP8 = mybir.dt.float8_e4m3fn
FP8X4 = mybir.dt.float8_e4m3fn_x4
ALU = mybir.AluOpType
ACT = mybir.ActivationFunctionType

P = 128
B = 4
H = 16
K = 2048
G = 4
TOK = 512
HR = 13
NX = 3


def tile_attention_pa_kernel(tc, query, wq_bytes, wq_scale, bq, cos, sin, out):
    nc = tc.nc
    with ExitStack() as ctx:
        const = ctx.enter_context(tc.tile_pool(name="const", bufs=1))
        work = ctx.enter_context(tc.tile_pool(name="work", bufs=3))
        psum = ctx.enter_context(tc.psum_pool(name="psum", bufs=2))

        ctx.enter_context(tc.manual_schedule())

        wq_bytes_sb = const.tile([P, H, K], U8, name="wq_bytes_sb")
        scl = const.tile([P, K], F32, name="scl")
        xq = const.tile([P, B, K], BF16, name="xq")
        craw = const.tile([P, 3, P], BF16, name="craw")
        scl_t = const.tile([P, G, 8], F32, name="scl_t")
        for g in range(G):
            nc.scalar.dma_start(
                out=scl_t[:, g, 0:4], in_=wq_scale.rearrange("o (g p t) -> g p (o t)", p=P, t=4)[g]
            )

        one = const.tile([P, 1], F32, name="one")
        nc.vector.memset(one[:], 1.0)
        first = const.tile([P, 1], F32, name="first")
        nc.scalar.activation(out=first[:], in_=one[:], func=ACT.Copy, scale=1.0)
        ident = const.tile([P, P], F32, name="ident")
        make_identity(nc, ident[:])
        nc.gpsimd.memset(craw[:, 2, :], 0.0)
        perm = const.tile([P, P], F32, name="perm")
        nc.gpsimd.tensor_copy(out=perm[:, 0:64], in_=ident[:, 64:128])
        nc.gpsimd.tensor_copy(out=perm[:, 64:128], in_=ident[:, 0:64])

        def load_w(h, c0=0, c1=K):
            nc.sync.dma_start(out=wq_bytes_sb[:, h, c0:c1], in_=wq_bytes[h * P : (h + 1) * P, c0:c1])

        def load_q(b, gp):
            cs = slice(gp * 1024, (gp + 1) * 1024)
            nc.sync.dma_start(out=xq[:, b, cs], in_=query[b, :, cs])

        load_w(HR)
        load_q(0, 0)
        load_w(0)
        for b in range(1, B):
            load_q(b, 0)
        load_w(1)
        load_w(HR + 1)
        for b in range(B):
            load_q(b, 1)
        load_w(2)
        load_w(3)
        nc.sync.dma_start(out=craw[:, 0, :], in_=cos[0, 0])
        nc.sync.dma_start(out=craw[:, 1, :], in_=sin[0, 0])
        nc.sync.dma_start(out=craw[0:H, 2, :], in_=bq.rearrange("(h d) -> h d", d=P))
        for h in (4, HR + 2):
            load_w(h)
        for h in range(5, HR):
            load_w(h)

        def spread_scales():
            for g in range(G):
                spread = psum.tile([P, 512], F32, name="spread", tag="tw", bufs=3)
                for t in range(4):
                    column = scl_t[:, g, t : t + 1]
                    nc.tensor.transpose(spread[:, t * P : (t + 1) * P], column.to_broadcast([P, P]), ident[:])
                nc.scalar.copy(
                    out=scl[:, g * 512 : (g + 1) * 512].rearrange("p (c t) -> p c t", t=4),
                    in_=spread[:].rearrange("p (t c) -> p c t", t=4),
                )

        stg = const.tile([P, 3, P], F32, name="stg")
        tab = const.tile([P, 3, P], F32, name="tab")

        def tables_raw():
            nc.scalar.copy(out=stg[:, 0, :], in_=craw[:, 0, :])
            nc.scalar.copy(out=stg[:, 1, 0:64], in_=craw[:, 1, 64:128])
            nc.scalar.activation(out=stg[:, 1, 64:128], in_=craw[:, 1, 0:64], func=ACT.Copy, scale=-1.0)
            nc.scalar.copy(out=stg[:, 2, :], in_=craw[:, 2, :])

        def tables():
            tps = psum.tile([P, 512], F32, name="tps", tag="tw", bufs=3)
            for i in range(3):
                nc.tensor.transpose(tps[:, i * P : (i + 1) * P], stg[:, i, :], ident[:])
            nc.scalar.copy(out=tab[:].rearrange("p a s -> p (a s)"), in_=tps[:, 0 : 3 * P])

        qg = const.tile([P, G * TOK * 4], BF16, name="qg", align_bytes=64)
        qcodes = const.tile([P, G * TOK], U32, name="qcodes", align_bytes=64)
        qscales = const.tile([P, G * TOK], U8, name="qscales", align_bytes=64)
        wcodes = const.tile([P, H, G * P], U32, name="wcodes", align_bytes=64)
        wscales = const.tile([P, H, G * P], U8, name="wscales", align_bytes=64)
        qg_words = qg[:].bitcast(F32).rearrange("p (g n u) -> p g n u", g=G, n=TOK, u=2)

        def transpose_pair(words, gp):
            tw = psum.tile([P, 512], F32, name="tw", tag="tw", bufs=3)
            for g2 in range(2):
                g = 2 * gp + g2
                for u in range(2):
                    nc.tensor.transpose(
                        tw[:, (2 * g2 + u) * P : (2 * g2 + u + 1) * P],
                        words[:, 256 * g + u : 256 * (g + 1) : 2],
                        ident[:],
                    )
            return tw[:].rearrange("p (g u r) -> p g r u", g=2, u=2)

        wb_of = {}
        wg_of = {}
        acc_of = {}
        uw_of = {}
        ot_of = {}

        def product(h, gp):
            if gp == 0:
                wb_of[h] = work.tile([P, K], BF16, name="wb", tag="wb", bufs=4)
            k0 = 1024 * gp
            cuts = (k0, k0 + 512, k0 + 1024) if h == 0 else (k0, k0 + 1024)
            for c0, c1 in zip(cuts[:-1], cuts[1:]):
                nc.vector.tensor_tensor(
                    out=wb_of[h][:, c0:c1],
                    in0=wq_bytes_sb[:, h, c0:c1].bitcast(FP8),
                    in1=scl[:, c0:c1],
                    op=ALU.mult,
                )

        def turn_w(h, gp):
            if gp == 0:
                wg_of[h] = work.tile([P, K], BF16, name="wg", tag="wg", align_bytes=64, bufs=4)
            wg_words = wg_of[h][:].bitcast(F32).rearrange("p (g r u) -> p g r u", g=G, u=2)
            src = transpose_pair(wb_of[h][:].bitcast(F32), gp)
            nc.scalar.copy(out=wg_words[:, 2 * gp : 2 * gp + 2, :, :], in_=src)

        def turn_q(b, gp):
            src = transpose_pair(xq[:, b, :].bitcast(F32), gp)
            nc.scalar.copy(out=qg_words[:, 2 * gp : 2 * gp + 2, b * P : (b + 1) * P, :], in_=src)

        def quant_q(gp):
            cols = slice(2 * gp * TOK, (2 * gp + 2) * TOK)
            nc.vector.quantize_mx(
                out=qcodes[:, cols].bitcast(FP8X4),
                scales=qscales[:, cols],
                in_=qg[:, 2 * gp * TOK * 4 : (2 * gp + 2) * TOK * 4],
            )

        def quant_w(h):
            nc.vector.quantize_mx(
                out=wcodes[:, h, :].bitcast(FP8X4),
                scales=wscales[:, h, :],
                in_=wg_of[h][:] if h < HR else xsingle[:],
            )

        def quant_early(gp):
            nc.vector.quantize_mx(
                out=xcodes[:, gp * 512 : (gp + 1) * 512].bitcast(FP8X4),
                scales=xscales[:, gp * 512 : (gp + 1) * 512],
                in_=xearly[:, gp * 2048 : (gp + 1) * 2048],
            )

        def multiply(h, passes=(0, 1, 2, 3)):
            if passes[0] == 0:
                acc_of[h] = psum.tile([P, TOK], F32, name="acc", tag="acc", bufs=3)
            for g in passes:
                if h in (HR, HR + 1):
                    cols = slice((2 * g + h - HR) * P, (2 * g + h - HR + 1) * P)
                    codes, scales = xcodes[:, cols], xscales[:, cols]
                else:
                    cols = slice(g * P, (g + 1) * P)
                    codes, scales = wcodes[:, h, cols], wscales[:, h, cols]
                nc.tensor.matmul_mx(
                    out=acc_of[h][:],
                    lhsT=codes.bitcast(FP8X4),
                    lhsT_scale=scales,
                    rhs=qcodes[:, g * TOK : (g + 1) * TOK].bitcast(FP8X4),
                    rhs_scale=qscales[:, g * TOK : (g + 1) * TOK],
                    start=(g == 0),
                    stop=(g == G - 1),
                )

        def rope(h, b0, nb):
            cs = slice(b0 * P, (b0 + nb) * P)
            uu = work.tile([P, nb * P], F32, name="uu", tag="uu", bufs=4)
            ww = work.tile([P, nb * P], F32, name="ww", tag="ww", bufs=4)
            for dst, a in ((uu, 0), (ww, 1)):
                nc.vector.scalar_tensor_tensor(
                    out=dst[:].rearrange("p (b s) -> p b s", b=nb),
                    in0=acc_of[h][:, cs].rearrange("p (b s) -> p b s", b=nb),
                    scalar=tab[:, 2, h : h + 1],
                    in1=tab[:, a, :].unsqueeze(1).to_broadcast([P, nb, P]),
                    op0=ALU.add,
                    op1=ALU.mult,
                )
            uw_of[(h, b0)] = (uu, ww)

        def turn_back(h, b0, nb, late=False):
            uu, ww = uw_of[(h, b0)]
            if late:
                ot = psum.tile([P, nb * P], F32, name="ot", tag="tw", bufs=3)
            else:
                ot = psum.tile([P, nb * P], F32, name="ot", tag="ot", bufs=2)
            for b in range(nb):
                cs = slice(b * P, (b + 1) * P)
                nc.tensor.matmul(
                    out=ot[:, cs], lhsT=uu[:, cs], rhs=ident[:], is_transpose=True, start=True, stop=False
                )
                nc.tensor.matmul(
                    out=ot[:, cs], lhsT=ww[:, cs], rhs=perm[:], is_transpose=True, start=False, stop=True
                )
            osb = work.tile([P, nb * P], F32, name="osb", tag="osb", bufs=8)
            nc.scalar.copy(out=osb[:], in_=ot[:])
            nc.sync.dma_start(
                out=out[b0 : b0 + nb, h, :, :].rearrange("b s d -> s b d"),
                in_=osb[:].rearrange("p (b d) -> p b d", b=nb),
            )

        xearly = const.tile([P, G * 2 * P * 4], BF16, name="xearly", align_bytes=64)
        xsingle = const.tile([P, K], BF16, name="xsingle", align_bytes=64)
        xcodes = const.tile([P, G * 2 * P], U32, name="xcodes", align_bytes=64)
        xscales = const.tile([P, G * 2 * P], U8, name="xscales", align_bytes=64)
        early = const.tile([P, G, 4, 2 * P], BF16, name="early")
        single = const.tile([P, G, 4, P], BF16, name="single")
        wc_of = {}

        def widen(r, on_vector):
            wc_of[r] = const.tile([P, K], BF16, name="wc%d" % r)
            src = wq_bytes_sb[:, HR + r, :].bitcast(FP8)
            if on_vector:
                nc.vector.tensor_copy(out=wc_of[r][:], in_=src)
            else:
                nc.scalar.copy(out=wc_of[r][:], in_=src)

        def turn_x(dst, pieces, width):
            tw = psum.tile([P, 512], F32, name="tw", tag="tw", bufs=3)
            col = 0
            for g, heads in pieces:
                for u in range(2):
                    for r in heads:
                        nc.tensor.transpose(
                            tw[:, col : col + P],
                            wc_of[r][:].bitcast(F32)[:, 256 * g + u : 256 * (g + 1) : 2],
                            ident[:],
                        )
                        col += P
            pairs = tw[:].bitcast(BF16).rearrange("p (q c e) -> p q c e", c=width, e=2)
            for i, (g, heads) in enumerate(pieces):
                for t in range(4):
                    nc.scalar.activation(
                        out=dst[:, g, t, :],
                        in_=pairs[:, 2 * i + t // 2, :, t % 2],
                        func=ACT.Copy,
                        scale=scl_t[:, g, t : t + 1],
                    )

        def weave_early(g):
            nc.scalar.copy(
                out=xearly[:, g * 1024 : (g + 1) * 1024].rearrange("p (c i t) -> p c t i", i=4, t=4),
                in_=early[:, g, :, :].rearrange("p t (c i) -> p c t i", i=4),
            )

        def weave_single(g):
            nc.scalar.copy(
                out=xsingle[:, g * 512 : (g + 1) * 512].rearrange("p (c i t) -> p c t i", i=4, t=4),
                in_=single[:, g, :, :].rearrange("p t (c i) -> p c t i", i=4),
            )

        def road(j):
            if 2 <= j < 6:
                turn_x(early, [(j - 2, (0, 1))], 2 * P)
            if 4 <= j < 7:
                weave_early(j - 4)
            if j == 6:
                weave_early(3)
            if j == 7:
                widen(2, False)
            if j in (8, 9):
                turn_x(single, [(2 * j - 16, (2,)), (2 * j - 15, (2,))], P)
            if j == 10:
                for g in range(G):
                    weave_single(g)

        def live(h):
            return 0 <= h < HR

        def finish(h, late=False):
            rope(h, 0, B)
            turn_back(h, 0, B, late)

        widen(0, True)
        spread_scales()
        for b in range(B):
            turn_q(b, 0)
        for j in range(HR + 3):
            if live(j):
                product(j, 0)
                turn_w(j, 0)
            if j == 2:
                turn_q(2, 1)
                turn_q(3, 1)
            if j == 4:
                multiply(1, (2, 3))
            if j >= 4 and live(j - 2) and j - 2 != HR - 1:
                multiply(j - 2, (2, 3))
            if live(j):
                product(j, 1)
                turn_w(j, 1)
            if j == 4:
                finish(0)
            elif j == 5:
                finish(1)
                finish(2)
            elif 6 <= j < HR + 2:
                finish(j - 3)
            elif j == HR + 2:
                for b0, nb in ((0, 2), (2, 1), (3, 1)):
                    rope(j - 3, b0, nb)
                    turn_back(j - 3, b0, nb, b0 != 2)
            if j in (9, 10):
                finish(HR + j - 9)
            if j == HR + 1:
                finish(HR + 2, True)
            if j in (1, 3):
                quant_q(j // 2)
            if j == 3:
                multiply(0, (2, 3))
            if live(j - 1):
                quant_w(j - 1)
                if j == HR:
                    multiply(j - 1)
                else:
                    multiply(j - 1, (0, 1))
            if j == 1:
                turn_q(0, 1)
                turn_q(1, 1)
                widen(1, True)
            if j == 2:
                tables_raw()
                tables()
            if j == 8:
                quant_early(0)
                quant_early(1)
            if j == 11:
                quant_w(HR + 2)
            if j in (8, 9, 11):
                multiply(HR + {8: 0, 9: 1, 11: 2}[j])
            road(j)
